import numpy as np
import ml_dtypes


def mxq(x, axis, fmt="e4m3"):
    dtype, down = {"e4m3": (ml_dtypes.float8_e4m3fn, 7), "e5m2": (ml_dtypes.float8_e5m2, 14)}[fmt]
    v = np.moveaxis(np.asarray(x, np.float32).astype(ml_dtypes.bfloat16).astype(np.float64), axis, -1)
    blocks = v.reshape(v.shape[:-1] + (-1, 32))
    amax = np.abs(blocks).max(-1, keepdims=True)
    byte = np.maximum(np.where(amax > 0, np.frexp(amax)[1] - 1 + 127, 0) - down, 1)
    scale = np.exp2(byte - 127.0)
    codes = (blocks / scale).astype(np.float32).astype(dtype).astype(np.float64)
    return np.moveaxis((codes * scale).reshape(v.shape), -1, axis)


WIDE = False


def mx_kscale(k):
    if not WIDE:
        return np.ones(k)
    levels = np.array([10, -10, 5, -5, 0])
    if k % 512:
        return np.exp2(np.random.permutation(np.resize(levels, k // 32))).repeat(32)
    a = np.empty((k // 512, 16))
    for p in range(k // 512):
        a[p, :8] = np.random.permutation(np.resize(levels, 8))
        for g in range(8):
            far = levels[np.abs(levels - a[p, g]) >= 10]
            a[p, g + 8] = far[np.random.randint(len(far))]
    return np.exp2(a.ravel()).repeat(32)


BF16 = ml_dtypes.bfloat16


def bf(x):
    return np.asarray(x, np.float32).astype(BF16)


def f64(x):
    return np.asarray(x).astype(np.float64)


B, N, D, LAYER_NUM = 4, 512, 512, 1


def setup_inputs():
    s = mx_kscale(N)[None, :, None]
    u = mx_kscale(D)
    x0 = bf(np.random.standard_normal((B, N, D)))
    w0 = bf(np.random.standard_normal((B, D, D)) * 1.2 / np.sqrt(D))
    b0 = bf(np.random.standard_normal((B, D)) * 0.5)
    g = bf(np.random.standard_normal((B, N, D)) * np.exp2(np.random.randint(-6, 1, (B, N, 1))) / s * u)
    z = f64(x0) @ f64(w0) + f64(b0)[:, None, :]
    item = np.concatenate([(f64(w0) / u).reshape(B, D * D), f64(b0)], axis=1)
    return {"user_emb": bf(f64(x0) * s), "item_emb": bf(item), "z": np.asarray(z, np.float32), "grad_out": g}


def reference(user_emb, item_emb, z, grad_out):
    x = f64(user_emb)
    item = f64(item_emb)
    nb = x.shape[0]
    W = item[:, :D * D].reshape(nb, D, D)
    dz = f64(grad_out) * (f64(z) > 0.0)
    dx = mxq(dz, 2, "e5m2") @ mxq(W, 2, "e4m3").transpose(0, 2, 1)
    dW = mxq(x, 1, "e4m3").transpose(0, 2, 1) @ mxq(dz, 1, "e5m2")
    db = dz.sum(axis=1)
    return dx, np.concatenate([dW.reshape(nb, D * D), db], axis=1)

@@ -1,0 +1,197 @@
+from contextlib import ExitStack
+
+import concourse.mybir as mybir
+from concourse.masks import make_identity
+
+B, N, D = 4, 512, 512
+P = 128
+J = 4
+HALF = 2 * D
+
+F32 = mybir.dt.float32
+BF16 = mybir.dt.bfloat16
+U32 = mybir.dt.uint32
+U8 = mybir.dt.uint8
+E4M3X4 = mybir.dt.float8_e4m3fn_x4
+E5M2X4 = mybir.dt.float8_e5m2_x4
+ALU = mybir.AluOpType
+
+FLOPS = 2 * 2 * B * N * D * D
+BYTES = B * N * D * (2 + 2 + 4 + 2 + 4 + 4) + B * D * 4
+
+
+def rows_of_4(flat):
+    return flat.rearrange("(p j) w -> p (j w)", j=J)
+
+
+def tile_can_v_kernel(tc, user_emb, item_emb, z, grad_out, out_0, out_1):
+    nc = tc.nc
+
+    with ExitStack() as ctx:
+        const = ctx.enter_context(tc.tile_pool(name="const", bufs=1))
+        loads = ctx.enter_context(tc.tile_pool(name="loads", bufs=B))
+        first = ctx.enter_context(tc.tile_pool(name="first", bufs=2))
+        work = ctx.enter_context(tc.tile_pool(name="work", bufs=2))
+        outs = ctx.enter_context(tc.tile_pool(name="outs", bufs=B))
+        ps_tr = ctx.enter_context(tc.psum_pool(name="ps_tr", bufs=3))
+        ps_out = ctx.enter_context(tc.psum_pool(name="ps_out", bufs=4))
+        ps_db = ctx.enter_context(tc.psum_pool(name="ps_db", bufs=1))
+        ctx.enter_context(tc.manual_schedule())
+
+        ident = const.tile([P, P], F32, name="ident")
+        make_identity(nc, ident[:])
+        ones = const.tile([P, 1], BF16, name="ones")
+        nc.gpsimd.memset(ones[:], 1.0)
+        db_cols = const.tile([P, J, P], F32, name="db_cols")
+        nc.gpsimd.memset(db_cols[:], 0.0)
+        db_row = const.tile([B, D], F32, name="db_row")
+        db_ps = ps_db.tile([P, J, B], F32, name="db_ps")
+
+        x_raw, w_raw, z_half, g_half = {}, {}, {}, {}
+
+        def load_x(b):
+            x_t = loads.tile([P, J * D], BF16, name="x_t")
+            nc.sync.dma_start(out=x_t[:], in_=rows_of_4(user_emb[b]))
+            x_raw[b] = x_t
+
+        def load_w(b):
+            w_t = loads.tile([P, J * D], BF16, name="w_t")
+            nc.sync.dma_start(out=w_t[:], in_=item_emb[b, 0 : D * D].rearrange("(p c) -> p c", p=P))
+            w_raw[b] = w_t
+
+        def load_gz(b):
+            g_t = loads.tile([P, J * D], BF16, name="g_t")
+            nc.sync.dma_start(out=g_t[:], in_=rows_of_4(grad_out[b]))
+            z_t = loads.tile([P, J * D], F32, name="z_t")
+            nc.sync.dma_start(out=z_t[:], in_=rows_of_4(z[b]))
+            for h in range(2):
+                g_half[b, h] = g_t[:, h * HALF : (h + 1) * HALF]
+                z_half[b, h] = z_t[:, h * HALF : (h + 1) * HALF]
+
+        load_x(0)
+        for h in range(2):
+            cols = slice(h * HALF, (h + 1) * HALF)
+            g_h = first.tile([P, HALF], BF16, name="g_h")
+            nc.sync.dma_start(out=g_h[:], in_=rows_of_4(grad_out[0])[:, cols])
+            z_h = first.tile([P, HALF], F32, name="z_h")
+            nc.sync.dma_start(out=z_h[:], in_=rows_of_4(z[0])[:, cols])
+            g_half[0, h] = g_h[:]
+            z_half[0, h] = z_h[:]
+        load_w(0)
+        for b in range(1, B):
+            load_gz(b)
+            load_x(b)
+            load_w(b)
+
+        def quantize(src, dtype, tag):
+            codes = work.tile([P, D], U32, name="codes_" + tag, align_bytes=64)
+            scales = work.tile([P, D], U8, name="scales_" + tag, align_bytes=64)
+            nc.vector.quantize_mx(out=codes[:].bitcast(dtype), scales=scales[:], in_=src[:])
+            return codes[:].bitcast(dtype), scales[:]
+
+        def transpose_half(src, h):
+            tr = ps_tr.tile([P, 2, 2, P], F32, name="tr")
+            words = src.bitcast(F32)
+            for jj in range(2):
+                w0 = (2 * h + jj) * D // 2
+                for u in range(2):
+                    nc.tensor.transpose(tr[:, jj, u, :], words[:, w0 + u : w0 + D // 2 : 2], ident[:])
+            return tr
+
+        for b in range(B):
+            dz = work.tile([P, J * D], BF16, name="dz", align_bytes=64)
+            dzf = work.tile([P, J * D], BF16, name="dzf", align_bytes=64)
+            wf = work.tile([P, J * D], BF16, name="wf", align_bytes=64)
+            xg = work.tile([P, J * D], BF16, name="xg", align_bytes=64)
+            dzg = work.tile([P, J * D], BF16, name="dzg", align_bytes=64)
+
+            def mask_half(h):
+                nc.vector.scalar_tensor_tensor(
+                    out=dz[:, h * HALF : (h + 1) * HALF],
+                    in0=z_half[b, h],
+                    scalar=0.0,
+                    in1=g_half[b, h],
+                    op0=ALU.is_gt,
+                    op1=ALU.mult,
+                )
+
+            def group_x():
+                nc.vector.tensor_copy(
+                    out=xg[:].rearrange("p (m q t) -> p m q t", m=J, t=J),
+                    in_=x_raw[b][:].rearrange("p (t q m) -> p m q t", t=J, m=J),
+                )
+
+            def group_dz():
+                nc.vector.tensor_copy(
+                    out=dzg[:].rearrange("p (e t) -> p e t", t=J),
+                    in_=dz[:].rearrange("p (t e) -> p e t", t=J),
+                )
+
+            if b == 0:
+                group_x()
+                xq = quantize(xg, E4M3X4, "x")
+            for h in range(2):
+                mask_half(h)
+                tr = transpose_half(dz[:], h)
+                nc.scalar.copy(
+                    out=dzf[:].bitcast(F32).rearrange("q (j p u) -> q j p u", j=J, u=2)[:, 2 * h : 2 * h + 2],
+                    in_=tr[:].rearrange("q j u p -> q j p u"),
+                )
+            for h in range(2):
+                tr = transpose_half(w_raw[b][:], h)
+                nc.scalar.copy(
+                    out=wf[:].bitcast(F32).rearrange("q (p j u) -> q p j u", j=J, u=2)[:, :, 2 * h : 2 * h + 2],
+                    in_=tr[:].rearrange("q j u p -> q p j u"),
+                )
+            if b > 0:
+                group_x()
+            group_dz()
+            for eb in range(J):
+                for j in range(J):
+                    c0 = j * D + eb * P
+                    nc.tensor.matmul(
+                        db_ps[:, eb, b : b + 1],
+                        lhsT=dz[:, c0 : c0 + P],
+                        rhs=ones[:],
+                        start=(j == 0),
+                        stop=(j == J - 1),
+                    )
+            if b > 0:
+                xq = quantize(xg, E4M3X4, "x")
+            dzq_tok = quantize(dzg, E5M2X4, "dzg")
+            if b > 0:
+                wq = quantize(wf, E4M3X4, "w")
+                dzq_feat = quantize(dzf, E5M2X4, "dzf")
+            else:
+                dzq_feat = quantize(dzf, E5M2X4, "dzf")
+                wq = quantize(wf, E4M3X4, "w")
+
+            def product(lhs, rhs, dst_tile):
+                for m in range(J):
+                    cols = slice(m * P, (m + 1) * P)
+                    acc = ps_out.tile([P, D], F32, name="acc")
+                    nc.tensor.matmul_mx(
+                        out=acc[:],
+                        lhsT=lhs[0][:, cols],
+                        lhsT_scale=lhs[1][:, cols],
+                        rhs=rhs[0],
+                        rhs_scale=rhs[1],
+                        start=True,
+                        stop=True,
+                    )
+                    nc.scalar.copy(out=dst_tile[:, m * D : (m + 1) * D], in_=acc[:])
+
+            if b == B - 1:
+                nc.scalar.copy(out=db_cols[:, :, 0:B], in_=db_ps[:])
+            o1 = outs.tile([P, J * D], F32, name="o1")
+            product(xq, dzq_tok, o1)
+            nc.sync.dma_start(out=out_1[b, 0 : D * D].rearrange("(p c) -> p c", p=P), in_=o1[:])
+            if b == B - 1:
+                db_tr = ps_tr.tile([P, D], F32, name="tr")
+                for eb in range(J):
+                    nc.tensor.transpose(db_tr[:, eb * P : (eb + 1) * P], db_cols[:, eb, :], ident[:])
+                nc.scalar.copy(out=db_row[:], in_=db_tr[0:B, :])
+                nc.sync.dma_start(out=out_1[:, D * D : D * D + D], in_=db_row[:])
+            o0 = outs.tile([P, J * D], F32, name="o0")
+            product(dzq_feat, wq, o0)
+            nc.sync.dma_start(out=rows_of_4(out_0[b]), in_=o0[:])

@@ -6,6 +6,7 @@ from concourse.masks import make_identity
 B, N, D = 4, 512, 512
 P = 128
 J = 4
+DB_N = 64
 HALF = 2 * D
 
 F32 = mybir.dt.float32
@@ -40,12 +41,11 @@ def tile_can_v_kernel(tc, user_emb, item_emb, z, grad_out, out_0, out_1):
 
         ident = const.tile([P, P], F32, name="ident")
         make_identity(nc, ident[:])
-        ones = const.tile([P, 1], BF16, name="ones")
+        ones = const.tile([P, DB_N], BF16, name="ones")
         nc.gpsimd.memset(ones[:], 1.0)
         db_cols = const.tile([P, J, P], F32, name="db_cols")
         nc.gpsimd.memset(db_cols[:], 0.0)
         db_row = const.tile([B, D], F32, name="db_row")
-        db_ps = ps_db.tile([P, J, B], F32, name="db_ps")
 
         x_raw, w_raw, z_half, g_half = {}, {}, {}, {}
 
@@ -78,16 +78,52 @@ def tile_can_v_kernel(tc, user_emb, item_emb, z, grad_out, out_0, out_1):
             g_half[0, h] = g_h[:]
             z_half[0, h] = z_h[:]
         load_w(0)
+        load_w(1)
         for b in range(1, B):
             load_gz(b)
             load_x(b)
-            load_w(b)
+            if b + 1 < B:
+                load_w(b + 1)
 
         def quantize(src, dtype, tag):
             codes = work.tile([P, D], U32, name="codes_" + tag, align_bytes=64)
             scales = work.tile([P, D], U8, name="scales_" + tag, align_bytes=64)
             nc.vector.quantize_mx(out=codes[:].bitcast(dtype), scales=scales[:], in_=src[:])
             return codes[:].bitcast(dtype), scales[:]
+
+        dz, dzf, wf, xg, dzg, o0, o1 = {}, {}, {}, {}, {}, {}, {}
+        xq, wq, dzq_tok, dzq_feat = {}, {}, {}, {}
+
+        def new_tiles(b):
+            dz_t = work.tile([P, J * D], BF16, name="dz_t", align_bytes=64)
+            dzf_t = work.tile([P, J * D], BF16, name="dzf_t", align_bytes=64)
+            xg_t = work.tile([P, J * D], BF16, name="xg_t", align_bytes=64)
+            dzg_t = work.tile([P, J * D], BF16, name="dzg_t", align_bytes=64)
+            o1_t = outs.tile([P, J * D], F32, name="o1_t")
+            o0_t = outs.tile([P, J * D], F32, name="o0_t")
+            dz[b], dzf[b], xg[b], dzg[b], o0[b], o1[b] = dz_t, dzf_t, xg_t, dzg_t, o0_t, o1_t
+
+        def mask_half(b, h):
+            nc.vector.scalar_tensor_tensor(
+                out=dz[b][:, h * HALF : (h + 1) * HALF],
+                in0=z_half[b, h],
+                scalar=0.0,
+                in1=g_half[b, h],
+                op0=ALU.is_gt,
+                op1=ALU.mult,
+            )
+
+        def group_x(b):
+            nc.vector.tensor_copy(
+                out=xg[b][:].rearrange("p (m c i t) -> p c m i t", m=J, i=2, t=J),
+                in_=x_raw[b][:].rearrange("p (t c i m) -> p c m i t", t=J, i=2, m=J),
+            )
+
+        def group_dz(b):
+            nc.vector.tensor_copy(
+                out=dzg[b][:].rearrange("p (c i t) -> p c t i", i=4, t=J),
+                in_=dz[b][:].rearrange("p (t c i) -> p c t i", i=4, t=J),
+            )
 
         def transpose_half(src, h):
             tr = ps_tr.tile([P, 2, 2, P], F32, name="tr")
@@ -98,100 +134,121 @@ def tile_can_v_kernel(tc, user_emb, item_emb, z, grad_out, out_0, out_1):
                     nc.tensor.transpose(tr[:, jj, u, :], words[:, w0 + u : w0 + D // 2 : 2], ident[:])
             return tr
 
-        for b in range(B):
-            dz = work.tile([P, J * D], BF16, name="dz", align_bytes=64)
-            dzf = work.tile([P, J * D], BF16, name="dzf", align_bytes=64)
-            wf = work.tile([P, J * D], BF16, name="wf", align_bytes=64)
-            xg = work.tile([P, J * D], BF16, name="xg", align_bytes=64)
-            dzg = work.tile([P, J * D], BF16, name="dzg", align_bytes=64)
+        def turn_dz(b, h):
+            tr = transpose_half(dz[b][:], h)
+            nc.scalar.copy(
+                out=dzf[b][:].bitcast(F32).rearrange("q (j p u) -> q j p u", j=J, u=2)[:, 2 * h : 2 * h + 2],
+                in_=tr[:].rearrange("q j u p -> q j p u"),
+            )
 
-            def mask_half(h):
-                nc.vector.scalar_tensor_tensor(
-                    out=dz[:, h * HALF : (h + 1) * HALF],
-                    in0=z_half[b, h],
-                    scalar=0.0,
-                    in1=g_half[b, h],
-                    op0=ALU.is_gt,
-                    op1=ALU.mult,
+        def turn_w(b, h):
+            if h == 0:
+                wf_t = work.tile([P, J * D], BF16, name="wf_t", align_bytes=64)
+                wf[b] = wf_t
+            tr = transpose_half(w_raw[b][:], h)
+            nc.scalar.copy(
+                out=wf[b][:].bitcast(F32).rearrange("q (p j u) -> q p j u", j=J, u=2)[:, :, 2 * h : 2 * h + 2],
+                in_=tr[:].rearrange("q j u p -> q p j u"),
+            )
+
+        db_ps = {}
+
+        def add_tokens(b, eb):
+            if eb == 0:
+                db_t = ps_db.tile([P, J, DB_N], F32, name="db_t")
+                db_ps[b] = db_t
+            for j in range(J):
+                c0 = j * D + eb * P
+                nc.tensor.matmul(
+                    db_ps[b][:, eb, :],
+                    lhsT=dz[b][:, c0 : c0 + P],
+                    rhs=ones[:],
+                    start=(j == 0),
+                    stop=(j == J - 1),
                 )
+            if eb == J - 1:
+                nc.scalar.copy(out=db_cols[:, :, b : b + 1], in_=db_ps[b][:, :, 0:1])
 
-            def group_x():
-                nc.vector.tensor_copy(
-                    out=xg[:].rearrange("p (m q t) -> p m q t", m=J, t=J),
-                    in_=x_raw[b][:].rearrange("p (t q m) -> p m q t", t=J, m=J),
-                )
+        def multiply(lhs, rhs, dst, m, copy):
+            cols = slice(m * P, (m + 1) * P)
+            acc = ps_out.tile([P, D], F32, name="acc")
+            nc.tensor.matmul_mx(
+                out=acc[:],
+                lhsT=lhs[0][:, cols],
+                lhsT_scale=lhs[1][:, cols],
+                rhs=rhs[0],
+                rhs_scale=rhs[1],
+                start=True,
+                stop=True,
+            )
+            copy(out=dst[:, m * D : (m + 1) * D], in_=acc[:])
 
-            def group_dz():
-                nc.vector.tensor_copy(
-                    out=dzg[:].rearrange("p (e t) -> p e t", t=J),
-                    in_=dz[:].rearrange("p (t e) -> p e t", t=J),
-                )
+        def dw_block(b, m, copy=nc.scalar.copy):
+            multiply(xq[b], dzq_tok[b], o1[b], m, copy)
 
-            if b == 0:
-                group_x()
-                xq = quantize(xg, E4M3X4, "x")
+        def dx_block(b, m, copy=nc.scalar.copy):
+            multiply(dzq_feat[b], wq[b], o0[b], m, copy)
+
+        def dw_hbm(b):
+            return out_1[b, 0 : D * D].rearrange("(p c) -> p c", p=P)
+
+        new_tiles(0)
+        group_x(0)
+        xq[0] = quantize(xg[0], E4M3X4, "x")
+        for h in range(2):
+            mask_half(0, h)
+            turn_dz(0, h)
+        for b in range(2):
             for h in range(2):
-                mask_half(h)
-                tr = transpose_half(dz[:], h)
-                nc.scalar.copy(
-                    out=dzf[:].bitcast(F32).rearrange("q (j p u) -> q j p u", j=J, u=2)[:, 2 * h : 2 * h + 2],
-                    in_=tr[:].rearrange("q j u p -> q j p u"),
-                )
+                turn_w(b, h)
+        for eb in range(J):
+            add_tokens(0, eb)
+        group_dz(0)
+        dzq_feat[0] = quantize(dzf[0], E5M2X4, "dzf")
+        dzq_tok[0] = quantize(dzg[0], E5M2X4, "dzg")
+        wq[0] = quantize(wf[0], E4M3X4, "w")
+
+        for b in range(1, B):
+            a = b - 1
+            new_tiles(b)
+            mask_half(b, 0)
+            mask_half(b, 1)
+            dx_block(a, 0)
+            dx_block(a, 1)
+            turn_dz(b, 0)
+            dx_block(a, 2)
+            turn_dz(b, 1)
+            dx_block(a, 3)
+            nc.sync.dma_start(out=rows_of_4(out_0[a]), in_=o0[a][:])
+            add_tokens(b, 0)
+            dw_block(a, 0)
+            if b + 1 < B:
+                turn_w(b + 1, 0)
+            add_tokens(b, 1)
+            dw_block(a, 1)
+            add_tokens(b, 2)
+            dw_block(a, 2)
+            if b + 1 < B:
+                turn_w(b + 1, 1)
+            add_tokens(b, 3)
+            dw_block(a, 3)
+            nc.sync.dma_start(out=dw_hbm(a), in_=o1[a][:])
+            group_x(b)
+            wq[b] = quantize(wf[b], E4M3X4, "w")
+            group_dz(b)
+            xq[b] = quantize(xg[b], E4M3X4, "x")
+            dzq_feat[b] = quantize(dzf[b], E5M2X4, "dzf")
+            dzq_tok[b] = quantize(dzg[b], E5M2X4, "dzg")
+
+        a = B - 1
+        db_tr = ps_tr.tile([P, D], F32, name="tr")
+        for eb in range(J):
+            nc.tensor.transpose(db_tr[:, eb * P : (eb + 1) * P], db_cols[:, eb, :], ident[:])
+        nc.scalar.copy(out=db_row[:], in_=db_tr[0:B, :])
+        nc.sync.dma_start(out=out_1[:, D * D : D * D + D], in_=db_row[:])
+        for block, dst, hbm in ((dx_block, o0[a], rows_of_4(out_0[a])), (dw_block, o1[a], dw_hbm(a))):
+            for m in range(J):
+                block(a, m, nc.scalar.copy if m < 2 else nc.vector.tensor_copy)
             for h in range(2):
-                tr = transpose_half(w_raw[b][:], h)
-                nc.scalar.copy(
-                    out=wf[:].bitcast(F32).rearrange("q (p j u) -> q p j u", j=J, u=2)[:, :, 2 * h : 2 * h + 2],
-                    in_=tr[:].rearrange("q j u p -> q p j u"),
-                )
-            if b > 0:
-                group_x()
-            group_dz()
-            for eb in range(J):
-                for j in range(J):
-                    c0 = j * D + eb * P
-                    nc.tensor.matmul(
-                        db_ps[:, eb, b : b + 1],
-                        lhsT=dz[:, c0 : c0 + P],
-                        rhs=ones[:],
-                        start=(j == 0),
-                        stop=(j == J - 1),
-                    )
-            if b > 0:
-                xq = quantize(xg, E4M3X4, "x")
-            dzq_tok = quantize(dzg, E5M2X4, "dzg")
-            if b > 0:
-                wq = quantize(wf, E4M3X4, "w")
-                dzq_feat = quantize(dzf, E5M2X4, "dzf")
-            else:
-                dzq_feat = quantize(dzf, E5M2X4, "dzf")
-                wq = quantize(wf, E4M3X4, "w")
-
-            def product(lhs, rhs, dst_tile):
-                for m in range(J):
-                    cols = slice(m * P, (m + 1) * P)
-                    acc = ps_out.tile([P, D], F32, name="acc")
-                    nc.tensor.matmul_mx(
-                        out=acc[:],
-                        lhsT=lhs[0][:, cols],
-                        lhsT_scale=lhs[1][:, cols],
-                        rhs=rhs[0],
-                        rhs_scale=rhs[1],
-                        start=True,
-                        stop=True,
-                    )
-                    nc.scalar.copy(out=dst_tile[:, m * D : (m + 1) * D], in_=acc[:])
-
-            if b == B - 1:
-                nc.scalar.copy(out=db_cols[:, :, 0:B], in_=db_ps[:])
-            o1 = outs.tile([P, J * D], F32, name="o1")
-            product(xq, dzq_tok, o1)
-            nc.sync.dma_start(out=out_1[b, 0 : D * D].rearrange("(p c) -> p c", p=P), in_=o1[:])
-            if b == B - 1:
-                db_tr = ps_tr.tile([P, D], F32, name="tr")
-                for eb in range(J):
-                    nc.tensor.transpose(db_tr[:, eb * P : (eb + 1) * P], db_cols[:, eb, :], ident[:])
-                nc.scalar.copy(out=db_row[:], in_=db_tr[0:B, :])
-                nc.sync.dma_start(out=out_1[:, D * D : D * D + D], in_=db_row[:])
-            o0 = outs.tile([P, J * D], F32, name="o0")
-            product(dzq_feat, wq, o0)
-            nc.sync.dma_start(out=rows_of_4(out_0[b]), in_=o0[:])
+                cols = slice(h * HALF, (h + 1) * HALF)
+                nc.sync.dma_start(out=hbm[:, cols], in_=dst[:, cols])

@@ -17,6 +17,8 @@ E4M3X4 = mybir.dt.float8_e4m3fn_x4
 E5M2X4 = mybir.dt.float8_e5m2_x4
 ALU = mybir.AluOpType
 
+ALIGN = 512
+
 FLOPS = 2 * 2 * B * N * D * D
 BYTES = B * N * D * (2 + 2 + 4 + 2 + 4 + 4) + B * D * 4
 
@@ -39,30 +41,30 @@ def tile_can_v_kernel(tc, user_emb, item_emb, z, grad_out, out_0, out_1):
         ps_db = ctx.enter_context(tc.psum_pool(name="ps_db", bufs=1))
         ctx.enter_context(tc.manual_schedule())
 
-        ident = const.tile([P, P], F32, name="ident")
+        ident = const.tile([P, P], F32, name="ident", align_bytes=ALIGN)
         make_identity(nc, ident[:])
         ones = const.tile([P, DB_N], BF16, name="ones")
         nc.gpsimd.memset(ones[:], 1.0)
-        db_cols = const.tile([P, J, P], F32, name="db_cols")
+        db_cols = const.tile([P, J, P], F32, name="db_cols", align_bytes=ALIGN)
         nc.gpsimd.memset(db_cols[:], 0.0)
-        db_row = const.tile([B, D], F32, name="db_row")
+        db_row = const.tile([B, D], F32, name="db_row", align_bytes=ALIGN)
 
         x_raw, w_raw, z_half, g_half = {}, {}, {}, {}
 
         def load_x(b):
-            x_t = loads.tile([P, J * D], BF16, name="x_t")
+            x_t = loads.tile([P, J * D], BF16, name="x_t", align_bytes=ALIGN)
             nc.sync.dma_start(out=x_t[:], in_=rows_of_4(user_emb[b]))
             x_raw[b] = x_t
 
         def load_w(b):
-            w_t = loads.tile([P, J * D], BF16, name="w_t")
+            w_t = loads.tile([P, J * D], BF16, name="w_t", align_bytes=ALIGN)
             nc.sync.dma_start(out=w_t[:], in_=item_emb[b, 0 : D * D].rearrange("(p c) -> p c", p=P))
             w_raw[b] = w_t
 
         def load_gz(b):
-            g_t = loads.tile([P, J * D], BF16, name="g_t")
+            g_t = loads.tile([P, J * D], BF16, name="g_t", align_bytes=ALIGN)
             nc.sync.dma_start(out=g_t[:], in_=rows_of_4(grad_out[b]))
-            z_t = loads.tile([P, J * D], F32, name="z_t")
+            z_t = loads.tile([P, J * D], F32, name="z_t", align_bytes=ALIGN)
             nc.sync.dma_start(out=z_t[:], in_=rows_of_4(z[b]))
             for h in range(2):
                 g_half[b, h] = g_t[:, h * HALF : (h + 1) * HALF]
@@ -71,9 +73,9 @@ def tile_can_v_kernel(tc, user_emb, item_emb, z, grad_out, out_0, out_1):
         load_x(0)
         for h in range(2):
             cols = slice(h * HALF, (h + 1) * HALF)
-            g_h = first.tile([P, HALF], BF16, name="g_h")
+            g_h = first.tile([P, HALF], BF16, name="g_h", align_bytes=ALIGN)
             nc.sync.dma_start(out=g_h[:], in_=rows_of_4(grad_out[0])[:, cols])
-            z_h = first.tile([P, HALF], F32, name="z_h")
+            z_h = first.tile([P, HALF], F32, name="z_h", align_bytes=ALIGN)
             nc.sync.dma_start(out=z_h[:], in_=rows_of_4(z[0])[:, cols])
             g_half[0, h] = g_h[:]
             z_half[0, h] = z_h[:]
@@ -86,8 +88,8 @@ def tile_can_v_kernel(tc, user_emb, item_emb, z, grad_out, out_0, out_1):
                 load_w(b + 1)
 
         def quantize(src, dtype, tag):
-            codes = work.tile([P, D], U32, name="codes_" + tag, align_bytes=64)
-            scales = work.tile([P, D], U8, name="scales_" + tag, align_bytes=64)
+            codes = work.tile([P, D], U32, name="codes_" + tag, align_bytes=ALIGN)
+            scales = work.tile([P, D], U8, name="scales_" + tag, align_bytes=ALIGN)
             nc.vector.quantize_mx(out=codes[:].bitcast(dtype), scales=scales[:], in_=src[:])
             return codes[:].bitcast(dtype), scales[:]
 
@@ -95,12 +97,12 @@ def tile_can_v_kernel(tc, user_emb, item_emb, z, grad_out, out_0, out_1):
         xq, wq, dzq_tok, dzq_feat = {}, {}, {}, {}
 
         def new_tiles(b):
-            dz_t = work.tile([P, J * D], BF16, name="dz_t", align_bytes=64)
-            dzf_t = work.tile([P, J * D], BF16, name="dzf_t", align_bytes=64)
-            xg_t = work.tile([P, J * D], BF16, name="xg_t", align_bytes=64)
-            dzg_t = work.tile([P, J * D], BF16, name="dzg_t", align_bytes=64)
-            o1_t = outs.tile([P, J * D], F32, name="o1_t")
-            o0_t = outs.tile([P, J * D], F32, name="o0_t")
+            dz_t = work.tile([P, J * D], BF16, name="dz_t", align_bytes=ALIGN)
+            dzf_t = work.tile([P, J * D], BF16, name="dzf_t", align_bytes=ALIGN)
+            xg_t = work.tile([P, J * D], BF16, name="xg_t", align_bytes=ALIGN)
+            dzg_t = work.tile([P, J * D], BF16, name="dzg_t", align_bytes=ALIGN)
+            o1_t = outs.tile([P, J * D], F32, name="o1_t", align_bytes=ALIGN)
+            o0_t = outs.tile([P, J * D], F32, name="o0_t", align_bytes=ALIGN)
             dz[b], dzf[b], xg[b], dzg[b], o0[b], o1[b] = dz_t, dzf_t, xg_t, dzg_t, o0_t, o1_t
 
         def mask_half(b, h):
@@ -143,7 +145,7 @@ def tile_can_v_kernel(tc, user_emb, item_emb, z, grad_out, out_0, out_1):
 
         def turn_w(b, h):
             if h == 0:
-                wf_t = work.tile([P, J * D], BF16, name="wf_t", align_bytes=64)
+                wf_t = work.tile([P, J * D], BF16, name="wf_t", align_bytes=ALIGN)
                 wf[b] = wf_t
             tr = transpose_half(w_raw[b][:], h)
             nc.scalar.copy(

from contextlib import ExitStack

import concourse.mybir as mybir
from concourse.masks import make_identity

B, N, D = 4, 512, 512
P = 128
J = 4
DB_N = 64
HALF = 2 * D

F32 = mybir.dt.float32
BF16 = mybir.dt.bfloat16
U32 = mybir.dt.uint32
U8 = mybir.dt.uint8
E4M3X4 = mybir.dt.float8_e4m3fn_x4
E5M2X4 = mybir.dt.float8_e5m2_x4
ALU = mybir.AluOpType

ALIGN = 512

FLOPS = 2 * 2 * B * N * D * D
BYTES = B * N * D * (2 + 2 + 4 + 2 + 4 + 4) + B * D * 4


def rows_of_4(flat):
    return flat.rearrange("(p j) w -> p (j w)", j=J)


def tile_can_v_kernel(tc, user_emb, item_emb, z, grad_out, out_0, out_1):
    nc = tc.nc

    with ExitStack() as ctx:
        const = ctx.enter_context(tc.tile_pool(name="const", bufs=1))
        loads = ctx.enter_context(tc.tile_pool(name="loads", bufs=B))
        first = ctx.enter_context(tc.tile_pool(name="first", bufs=2))
        work = ctx.enter_context(tc.tile_pool(name="work", bufs=2))
        outs = ctx.enter_context(tc.tile_pool(name="outs", bufs=B))
        ps_tr = ctx.enter_context(tc.psum_pool(name="ps_tr", bufs=3))
        ps_out = ctx.enter_context(tc.psum_pool(name="ps_out", bufs=4))
        ps_db = ctx.enter_context(tc.psum_pool(name="ps_db", bufs=1))
        ctx.enter_context(tc.manual_schedule())

        ident = const.tile([P, P], F32, name="ident", align_bytes=ALIGN)
        make_identity(nc, ident[:])
        ones = const.tile([P, DB_N], BF16, name="ones")
        nc.gpsimd.memset(ones[:], 1.0)
        db_cols = const.tile([P, J, P], F32, name="db_cols", align_bytes=ALIGN)
        nc.gpsimd.memset(db_cols[:], 0.0)
        db_row = const.tile([B, D], F32, name="db_row", align_bytes=ALIGN)

        x_raw, w_raw, z_half, g_half = {}, {}, {}, {}

        def load_x(b):
            x_t = loads.tile([P, J * D], BF16, name="x_t", align_bytes=ALIGN)
            nc.sync.dma_start(out=x_t[:], in_=rows_of_4(user_emb[b]))
            x_raw[b] = x_t

        def load_w(b):
            w_t = loads.tile([P, J * D], BF16, name="w_t", align_bytes=ALIGN)
            nc.sync.dma_start(out=w_t[:], in_=item_emb[b, 0 : D * D].rearrange("(p c) -> p c", p=P))
            w_raw[b] = w_t

        def load_gz(b):
            g_t = loads.tile([P, J * D], BF16, name="g_t", align_bytes=ALIGN)
            nc.sync.dma_start(out=g_t[:], in_=rows_of_4(grad_out[b]))
            z_t = loads.tile([P, J * D], F32, name="z_t", align_bytes=ALIGN)
            nc.sync.dma_start(out=z_t[:], in_=rows_of_4(z[b]))
            for h in range(2):
                g_half[b, h] = g_t[:, h * HALF : (h + 1) * HALF]
                z_half[b, h] = z_t[:, h * HALF : (h + 1) * HALF]

        load_x(0)
        for h in range(2):
            cols = slice(h * HALF, (h + 1) * HALF)
            g_h = first.tile([P, HALF], BF16, name="g_h", align_bytes=ALIGN)
            nc.sync.dma_start(out=g_h[:], in_=rows_of_4(grad_out[0])[:, cols])
            z_h = first.tile([P, HALF], F32, name="z_h", align_bytes=ALIGN)
            nc.sync.dma_start(out=z_h[:], in_=rows_of_4(z[0])[:, cols])
            g_half[0, h] = g_h[:]
            z_half[0, h] = z_h[:]
        load_w(0)
        load_w(1)
        for b in range(1, B):
            load_gz(b)
            load_x(b)
            if b + 1 < B:
                load_w(b + 1)

        def quantize(src, dtype, tag):
            codes = work.tile([P, D], U32, name="codes_" + tag, align_bytes=ALIGN)
            scales = work.tile([P, D], U8, name="scales_" + tag, align_bytes=ALIGN)
            nc.vector.quantize_mx(out=codes[:].bitcast(dtype), scales=scales[:], in_=src[:])
            return codes[:].bitcast(dtype), scales[:]

        dz, dzf, wf, xg, dzg, o0, o1 = {}, {}, {}, {}, {}, {}, {}
        xq, wq, dzq_tok, dzq_feat = {}, {}, {}, {}

        def new_tiles(b):
            dz_t = work.tile([P, J * D], BF16, name="dz_t", align_bytes=ALIGN)
            dzf_t = work.tile([P, J * D], BF16, name="dzf_t", align_bytes=ALIGN)
            xg_t = work.tile([P, J * D], BF16, name="xg_t", align_bytes=ALIGN)
            dzg_t = work.tile([P, J * D], BF16, name="dzg_t", align_bytes=ALIGN)
            o1_t = outs.tile([P, J * D], F32, name="o1_t", align_bytes=ALIGN)
            o0_t = outs.tile([P, J * D], F32, name="o0_t", align_bytes=ALIGN)
            dz[b], dzf[b], xg[b], dzg[b], o0[b], o1[b] = dz_t, dzf_t, xg_t, dzg_t, o0_t, o1_t

        def mask_half(b, h):
            nc.vector.scalar_tensor_tensor(
                out=dz[b][:, h * HALF : (h + 1) * HALF],
                in0=z_half[b, h],
                scalar=0.0,
                in1=g_half[b, h],
                op0=ALU.is_gt,
                op1=ALU.mult,
            )

        def group_x(b):
            nc.vector.tensor_copy(
                out=xg[b][:].rearrange("p (m c i t) -> p c m i t", m=J, i=2, t=J),
                in_=x_raw[b][:].rearrange("p (t c i m) -> p c m i t", t=J, i=2, m=J),
            )

        def group_dz(b):
            nc.vector.tensor_copy(
                out=dzg[b][:].rearrange("p (c i t) -> p c t i", i=4, t=J),
                in_=dz[b][:].rearrange("p (t c i) -> p c t i", i=4, t=J),
            )

        def transpose_half(src, h):
            tr = ps_tr.tile([P, 2, 2, P], F32, name="tr")
            words = src.bitcast(F32)
            for jj in range(2):
                w0 = (2 * h + jj) * D // 2
                for u in range(2):
                    nc.tensor.transpose(tr[:, jj, u, :], words[:, w0 + u : w0 + D // 2 : 2], ident[:])
            return tr

        def turn_dz(b, h):
            tr = transpose_half(dz[b][:], h)
            nc.scalar.copy(
                out=dzf[b][:].bitcast(F32).rearrange("q (j p u) -> q j p u", j=J, u=2)[:, 2 * h : 2 * h + 2],
                in_=tr[:].rearrange("q j u p -> q j p u"),
            )

        def turn_w(b, h):
            if h == 0:
                wf_t = work.tile([P, J * D], BF16, name="wf_t", align_bytes=ALIGN)
                wf[b] = wf_t
            tr = transpose_half(w_raw[b][:], h)
            nc.scalar.copy(
                out=wf[b][:].bitcast(F32).rearrange("q (p j u) -> q p j u", j=J, u=2)[:, :, 2 * h : 2 * h + 2],
                in_=tr[:].rearrange("q j u p -> q p j u"),
            )

        db_ps = {}

        def add_tokens(b, eb):
            if eb == 0:
                db_t = ps_db.tile([P, J, DB_N], F32, name="db_t")
                db_ps[b] = db_t
            for j in range(J):
                c0 = j * D + eb * P
                nc.tensor.matmul(
                    db_ps[b][:, eb, :],
                    lhsT=dz[b][:, c0 : c0 + P],
                    rhs=ones[:],
                    start=(j == 0),
                    stop=(j == J - 1),
                )
            if eb == J - 1:
                nc.scalar.copy(out=db_cols[:, :, b : b + 1], in_=db_ps[b][:, :, 0:1])

        def multiply(lhs, rhs, dst, m, copy):
            cols = slice(m * P, (m + 1) * P)
            acc = ps_out.tile([P, D], F32, name="acc")
            nc.tensor.matmul_mx(
                out=acc[:],
                lhsT=lhs[0][:, cols],
                lhsT_scale=lhs[1][:, cols],
                rhs=rhs[0],
                rhs_scale=rhs[1],
                start=True,
                stop=True,
            )
            copy(out=dst[:, m * D : (m + 1) * D], in_=acc[:])

        def dw_block(b, m, copy=nc.scalar.copy):
            multiply(xq[b], dzq_tok[b], o1[b], m, copy)

        def dx_block(b, m, copy=nc.scalar.copy):
            multiply(dzq_feat[b], wq[b], o0[b], m, copy)

        def dw_hbm(b):
            return out_1[b, 0 : D * D].rearrange("(p c) -> p c", p=P)

        new_tiles(0)
        group_x(0)
        xq[0] = quantize(xg[0], E4M3X4, "x")
        for h in range(2):
            mask_half(0, h)
            turn_dz(0, h)
        for b in range(2):
            for h in range(2):
                turn_w(b, h)
        for eb in range(J):
            add_tokens(0, eb)
        group_dz(0)
        dzq_feat[0] = quantize(dzf[0], E5M2X4, "dzf")
        dzq_tok[0] = quantize(dzg[0], E5M2X4, "dzg")
        wq[0] = quantize(wf[0], E4M3X4, "w")

        for b in range(1, B):
            a = b - 1
            new_tiles(b)
            mask_half(b, 0)
            mask_half(b, 1)
            dx_block(a, 0)
            dx_block(a, 1)
            turn_dz(b, 0)
            dx_block(a, 2)
            turn_dz(b, 1)
            dx_block(a, 3)
            nc.sync.dma_start(out=rows_of_4(out_0[a]), in_=o0[a][:])
            add_tokens(b, 0)
            dw_block(a, 0)
            if b + 1 < B:
                turn_w(b + 1, 0)
            add_tokens(b, 1)
            dw_block(a, 1)
            add_tokens(b, 2)
            dw_block(a, 2)
            if b + 1 < B:
                turn_w(b + 1, 1)
            add_tokens(b, 3)
            dw_block(a, 3)
            nc.sync.dma_start(out=dw_hbm(a), in_=o1[a][:])
            group_x(b)
            wq[b] = quantize(wf[b], E4M3X4, "w")
            group_dz(b)
            xq[b] = quantize(xg[b], E4M3X4, "x")
            dzq_feat[b] = quantize(dzf[b], E5M2X4, "dzf")
            dzq_tok[b] = quantize(dzg[b], E5M2X4, "dzg")

        a = B - 1
        db_tr = ps_tr.tile([P, D], F32, name="tr")
        for eb in range(J):
            nc.tensor.transpose(db_tr[:, eb * P : (eb + 1) * P], db_cols[:, eb, :], ident[:])
        nc.scalar.copy(out=db_row[:], in_=db_tr[0:B, :])
        nc.sync.dma_start(out=out_1[:, D * D : D * D + D], in_=db_row[:])
        for block, dst, hbm in ((dx_block, o0[a], rows_of_4(out_0[a])), (dw_block, o1[a], dw_hbm(a))):
            for m in range(J):
                block(a, m, nc.scalar.copy if m < 2 else nc.vector.tensor_copy)
            for h in range(2):
                cols = slice(h * HALF, (h + 1) * HALF)
                nc.sync.dma_start(out=hbm[:, cols], in_=dst[:, cols])
